import numpy as np
import ml_dtypes


def mxq(x, axis, fmt="e4m3"):
    dtype, down = {"e4m3": (ml_dtypes.float8_e4m3fn, 7), "e5m2": (ml_dtypes.float8_e5m2, 14)}[fmt]
    v = np.moveaxis(np.asarray(x, np.float32).astype(ml_dtypes.bfloat16).astype(np.float64), axis, -1)
    blocks = v.reshape(v.shape[:-1] + (-1, 32))
    amax = np.abs(blocks).max(-1, keepdims=True)
    byte = np.maximum(np.where(amax > 0, np.frexp(amax)[1] - 1 + 127, 0) - down, 1)
    scale = np.exp2(byte - 127.0)
    codes = (blocks / scale).astype(np.float32).astype(dtype).astype(np.float64)
    return np.moveaxis((codes * scale).reshape(v.shape), -1, axis)


WIDE = False


def mx_kscale(k):
    if not WIDE:
        return np.ones(k)
    levels = np.array([10, -10, 5, -5, 0])
    a = np.random.permutation(np.resize(levels, k // 512 * 4)).reshape(k // 512, 4)
    idx = np.arange(k)
    return np.exp2(a[idx // 512, idx % 128 // 32])


BF16 = ml_dtypes.bfloat16


def bf(x):
    return np.asarray(x, np.float32).astype(BF16)


def f64(x):
    return np.asarray(x).astype(np.float64)


E2M1 = np.array([0.0, 0.5, 1.0, 1.5, 2.0, 3.0, 4.0, 6.0, -0.0, -0.5, -1.0, -1.5, -2.0, -3.0, -4.0, -6.0])


def pack_weight(w, fmt):
    k, n = w.shape
    w = f64(bf(w)).reshape(k // 32, 32, n)
    amax = np.abs(w).max(1)
    if fmt == "e4m3":
        byte = np.frexp(amax)[1] - 1 + 127 - 7
    else:
        mant, ex = np.frexp(amax / 6.0)
        byte = np.where(mant > 0.5, ex, ex - 1) + 127
    byte = np.clip(np.where(amax > 0, byte, 1), 1, 254)
    scaled = (w * np.exp2(127.0 - byte)[:, None, :]).reshape(k, n).astype(np.float32)
    by_word = np.ascontiguousarray(scaled.reshape(k // 512, 128, 4, n).transpose(0, 1, 3, 2))
    if fmt == "e4m3":
        words = by_word.astype(ml_dtypes.float8_e4m3fn).view(np.uint8)
    else:
        c = by_word.astype(ml_dtypes.float4_e2m1fn).view(np.uint8) & 0xF
        words = c[..., 0::2] | (c[..., 1::2] << 4)
    return np.ascontiguousarray(words), np.ascontiguousarray(byte.astype(np.uint8).reshape(k // 512, 16, n))


def unpack_weight(words, scales, fmt):
    g, p, n, _ = words.shape
    if fmt == "e4m3":
        vals = np.ascontiguousarray(words).view(ml_dtypes.float8_e4m3fn).astype(np.float64)
    else:
        nib = np.empty((g, p, n, 4), np.uint8)
        nib[..., 0::2] = words & 0xF
        nib[..., 1::2] = words >> 4
        vals = E2M1[nib]
    vals = vals * np.repeat(np.exp2(scales.astype(np.float64) - 127.0), 8, axis=1)[..., None]
    return vals.transpose(0, 1, 3, 2).reshape(g * 512, n)

def pack4(w):
    words, scales = pack_weight(w, "e2m1")
    return words.reshape(words.shape[0], 128, -1), scales


def unpack4(words, scales):
    return unpack_weight(words.reshape(words.shape[0], 128, -1, 2), scales, "e2m1")


B, L, N, HID, H, D = 1, 128, 384, 1536, 12, 128


def apply_rope(x, rope):
    xp = x.reshape(x.shape[:-1] + (D // 2, 2))
    rp = rope[:, None].reshape(rope.shape[0], 1, rope.shape[1], D // 2, 2)
    cos, sin = rp[..., 0], rp[..., 1]
    x0, x1 = xp[..., 0], xp[..., 1]
    out = np.stack([x0 * cos - x1 * sin, x1 * cos + x0 * sin], axis=-1)
    return out.reshape(x.shape)


def setup_inputs():
    s = mx_kscale(HID)
    img = bf(np.random.standard_normal((B, N, HID)) * s)
    rope = bf(np.random.standard_normal((B, N, D)))
    w = np.random.standard_normal((3 * H * D, HID)) / np.sqrt(HID) / s
    words, scales = pack4(np.ascontiguousarray(w.T))
    return {"img": img,
            "rope": rope,
            "W_img_qkv_words": words,
            "W_img_qkv_scales": scales}


def reference(img, rope, W_img_qkv_words, W_img_qkv_scales):
    y = mxq(f64(img), 2, "e4m3") @ unpack4(W_img_qkv_words, W_img_qkv_scales)
    y = y.reshape(B, N, 3, H, D).transpose(2, 0, 3, 1, 4)
    r = f64(rope)
    return apply_rope(y[0], r), apply_rope(y[1], r), y[2]

@@ -1,0 +1,150 @@
+from contextlib import ExitStack
+
+import concourse.mybir as mybir
+from concourse.masks import make_identity
+
+F32 = mybir.dt.float32
+BF16 = mybir.dt.bfloat16
+I32 = mybir.dt.int32
+U32 = mybir.dt.uint32
+U8 = mybir.dt.uint8
+FP8X4 = mybir.dt.float8_e4m3fn_x4
+FP4X4 = mybir.dt.float4_e2m1fn_x4
+MULT = mybir.AluOpType.mult
+ADD = mybir.AluOpType.add
+
+P = 128
+TOKENS = 384
+HID = 1536
+HEADS = 12
+D = 128
+PAIRS = D // 2
+PARTS = 3
+
+K_PASS = 512
+PASSES = HID // K_PASS
+TOKEN_TILES = TOKENS // P
+GROUP_COLS = 512
+GROUP_HEADS = GROUP_COLS // D
+GROUPS_PER_PART = HEADS // GROUP_HEADS
+PART_COLS = HEADS * D
+
+FLOPS = 2 * TOKENS * HID * PARTS * PART_COLS
+
+
+def column_groups_in_turn():
+    order = []
+    for turn in range(GROUPS_PER_PART):
+        order.extend([2 * turn, 2 * turn + 1, 2 * GROUPS_PER_PART + turn])
+    return order
+
+
+def tile_jointattention_pa_kernel(tc, img, rope, w_words, w_scales, out_q, out_k, out_v):
+    nc = tc.nc
+    outs = (out_q, out_k, out_v)
+    with ExitStack() as ctx:
+        keep = ctx.enter_context(tc.tile_pool(name="keep", bufs=1))
+        stages = ctx.enter_context(tc.tile_pool(name="stages", bufs=4))
+        crosses = ctx.enter_context(tc.tile_pool(name="crosses", bufs=3))
+        psum = ctx.enter_context(tc.psum_pool(name="psum", bufs=8))
+
+        x_sb = keep.tile([P, TOKEN_TILES, HID], BF16)
+        rope_sb = keep.tile([P, TOKEN_TILES, D], BF16)
+        ident = keep.tile([P, P], F32)
+        grouped = keep.tile([P, TOKEN_TILES * PASSES, K_PASS], BF16, align_bytes=64)
+        x_codes = keep.tile([P, TOKEN_TILES * PASSES, P], U32, align_bytes=64)
+        x_scales = keep.tile([P, TOKEN_TILES * PASSES, P], U8, align_bytes=64)
+        w_sb = keep.tile([P, PARTS * GROUPS_PER_PART, PASSES, 2 * GROUP_COLS], U8, align_bytes=64)
+        w_planes = keep.tile([P, PARTS, PASSES, PART_COLS], U8, align_bytes=64)
+
+        for part in range(PARTS):
+            nc.vector.memset(w_planes[:, part].bitcast(I32), 0)
+        make_identity(nc, ident[:])
+
+        img_rows = img[0].rearrange("(p j) k -> p j k", j=TOKEN_TILES)
+        for j in range(TOKEN_TILES):
+            nc.sync.dma_start(out=x_sb[:, j, :], in_=img_rows[:, j, :])
+        nc.scalar.dma_start(out=rope_sb[:], in_=rope[0].rearrange("(p j) d -> p j d", j=TOKEN_TILES))
+
+        words_by_partition = w_words.rearrange("g p b -> p g b")
+        scales_by_row = w_scales.rearrange("g q n -> q g n")
+        parts_loaded = []
+        for c in column_groups_in_turn():
+            part = c // GROUPS_PER_PART
+            if part not in parts_loaded:
+                parts_loaded.append(part)
+                for q in range(8):
+                    first = 32 * (q // 4) + q % 4
+                    nc.sync.dma_start(
+                        out=w_planes[first:P:64, part].bitcast(I32),
+                        in_=scales_by_row[q:16:8, :, part * PART_COLS : (part + 1) * PART_COLS].bitcast(I32),
+                    )
+            nc.sync.dma_start(
+                out=w_sb[:, c].bitcast(I32),
+                in_=words_by_partition[:, :, c * 2 * GROUP_COLS : (c + 1) * 2 * GROUP_COLS].bitcast(I32),
+            )
+
+        x_words = x_sb[:].bitcast(F32)
+        for j in range(TOKEN_TILES):
+            for g in range(PASSES):
+                unit = j * PASSES + g
+                flipped = psum.tile([P, GROUP_COLS], F32, tag="bank")
+                for u in range(2):
+                    nc.tensor.transpose(
+                        flipped[:, u * P : (u + 1) * P],
+                        x_words[:, j, 256 * g + u : 256 * (g + 1) : 2],
+                        ident[:],
+                    )
+                nc.scalar.copy(
+                    out=grouped[:, unit, :].bitcast(F32).rearrange("p (r u) -> p r u", u=2),
+                    in_=flipped[:, 0 : 2 * P].rearrange("p (u r) -> p r u", u=2),
+                )
+                nc.vector.quantize_mx(
+                    out=x_codes[:, unit, :].bitcast(FP8X4),
+                    scales=x_scales[:, unit, :],
+                    in_=grouped[:, unit, :],
+                )
+
+        for c in column_groups_in_turn():
+            part = c // GROUPS_PER_PART
+            turn = c % GROUPS_PER_PART
+            rotated = part < 2
+            stage = stages.tile([P, GROUP_HEADS, TOKEN_TILES, D], F32)
+            if rotated:
+                cross = crosses.tile([P, 2, GROUP_HEADS, TOKEN_TILES, PAIRS], F32)
+            for j in range(TOKEN_TILES):
+                acc = psum.tile([P, GROUP_COLS], F32, tag="bank")
+                for g in range(PASSES):
+                    nc.tensor.matmul_mx(
+                        out=acc[:],
+                        lhsT=x_codes[:, j * PASSES + g, :].bitcast(FP8X4),
+                        lhsT_scale=x_scales[:, j * PASSES + g, :],
+                        rhs=w_sb[:, c, g, :].bitcast(FP4X4),
+                        rhs_scale=w_planes[:, part, g, turn * GROUP_COLS : (turn + 1) * GROUP_COLS],
+                        start=(g == 0),
+                        stop=(g == PASSES - 1),
+                    )
+                if not rotated:
+                    nc.scalar.copy(out=stage[:, :, j, :], in_=acc[:].rearrange("p (h d) -> p h d", d=D))
+                    continue
+                y_pairs = acc[:].rearrange("p (h i e) -> p h i e", h=GROUP_HEADS, e=2)
+                rope_pairs = rope_sb[:, j, :].rearrange("p (i e) -> p i e", e=2)
+                cos = rope_pairs[:, :, 0:1].unsqueeze(1).to_broadcast([P, GROUP_HEADS, PAIRS, 2])
+                sin = rope_pairs[:, :, 1].unsqueeze(1).to_broadcast([P, GROUP_HEADS, PAIRS])
+                nc.vector.tensor_tensor(
+                    out=stage[:, :, j, :].rearrange("p h (i e) -> p h i e", e=2), in0=y_pairs, in1=cos, op=MULT
+                )
+                nc.vector.scalar_tensor_tensor(
+                    out=cross[:, 0, :, j, :], in0=y_pairs[:, :, :, 1], scalar=-1.0, in1=sin, op0=MULT, op1=MULT
+                )
+                nc.vector.tensor_tensor(out=cross[:, 1, :, j, :], in0=y_pairs[:, :, :, 0], in1=sin, op=MULT)
+            if rotated:
+                stage_pairs = stage[:].rearrange("p h j (i e) -> p (h j i) e", e=2)
+                nc.gpsimd.tensor_tensor(
+                    out=stage_pairs, in0=stage_pairs, in1=cross[:].rearrange("p e h j i -> p (h j i) e"), op=ADD
+                )
+            heads = outs[part][0, turn * GROUP_HEADS : (turn + 1) * GROUP_HEADS]
+            nc.sync.dma_start(
+                out=heads.rearrange("h (p j) d -> p h (j d)", j=TOKEN_TILES),
+                in_=stage[:].rearrange("p h j d -> p h (j d)"),
+            )

@@ -45,44 +45,53 @@ def tile_jointattention_pa_kernel(tc, img, rope, w_words, w_scales, out_q, out_k
     with ExitStack() as ctx:
         keep = ctx.enter_context(tc.tile_pool(name="keep", bufs=1))
         stages = ctx.enter_context(tc.tile_pool(name="stages", bufs=4))
-        crosses = ctx.enter_context(tc.tile_pool(name="crosses", bufs=3))
+        products = ctx.enter_context(tc.tile_pool(name="products", bufs=4))
         psum = ctx.enter_context(tc.psum_pool(name="psum", bufs=8))
 
         x_sb = keep.tile([P, TOKEN_TILES, HID], BF16)
-        rope_sb = keep.tile([P, TOKEN_TILES, D], BF16)
+        table = keep.tile([P, TOKEN_TILES, 2, D], BF16)
         ident = keep.tile([P, P], F32)
         grouped = keep.tile([P, TOKEN_TILES * PASSES, K_PASS], BF16, align_bytes=64)
         x_codes = keep.tile([P, TOKEN_TILES * PASSES, P], U32, align_bytes=64)
         x_scales = keep.tile([P, TOKEN_TILES * PASSES, P], U8, align_bytes=64)
         w_sb = keep.tile([P, PARTS * GROUPS_PER_PART, PASSES, 2 * GROUP_COLS], U8, align_bytes=64)
-        w_planes = keep.tile([P, PARTS, PASSES, PART_COLS], U8, align_bytes=64)
+        w_planes = []
+        for part in range(PARTS):
+            planes = keep.tile([P, PASSES, PART_COLS], U8, align_bytes=64, name="planes%d" % part)
+            w_planes.append(planes)
 
         for part in range(PARTS):
-            nc.vector.memset(w_planes[:, part].bitcast(I32), 0)
+            nc.vector.memset(w_planes[part][:].bitcast(I32), 0)
         make_identity(nc, ident[:])
 
         img_rows = img[0].rearrange("(p j) k -> p j k", j=TOKEN_TILES)
         for j in range(TOKEN_TILES):
             nc.sync.dma_start(out=x_sb[:, j, :], in_=img_rows[:, j, :])
-        nc.scalar.dma_start(out=rope_sb[:], in_=rope[0].rearrange("(p j) d -> p j d", j=TOKEN_TILES))
+        nc.scalar.dma_start(out=table[:, :, 0, :], in_=rope[0].rearrange("(p j) d -> p j d", j=TOKEN_TILES))
+        table_pairs = table[:].rearrange("p j e (i f) -> p j e i f", f=2)
+        nc.gpsimd.tensor_scalar(
+            out=table_pairs[:, :, 1, :, 0], in0=table_pairs[:, :, 0, :, 1], scalar1=-1.0, scalar2=0.0, op0=MULT, op1=ADD
+        )
+        nc.gpsimd.tensor_scalar(
+            out=table_pairs[:, :, 1, :, 1], in0=table_pairs[:, :, 0, :, 0], scalar1=1.0, scalar2=0.0, op0=MULT, op1=ADD
+        )
 
         words_by_partition = w_words.rearrange("g p b -> p g b")
         scales_by_row = w_scales.rearrange("g q n -> q g n")
         parts_loaded = []
         for c in column_groups_in_turn():
             part = c // GROUPS_PER_PART
-            if part not in parts_loaded:
-                parts_loaded.append(part)
-                for q in range(8):
-                    first = 32 * (q // 4) + q % 4
-                    nc.sync.dma_start(
-                        out=w_planes[first:P:64, part].bitcast(I32),
-                        in_=scales_by_row[q:16:8, :, part * PART_COLS : (part + 1) * PART_COLS].bitcast(I32),
-                    )
             nc.sync.dma_start(
                 out=w_sb[:, c].bitcast(I32),
                 in_=words_by_partition[:, :, c * 2 * GROUP_COLS : (c + 1) * 2 * GROUP_COLS].bitcast(I32),
             )
+            if part not in parts_loaded:
+                parts_loaded.append(part)
+                for r in range(4):
+                    nc.sync.dma_start(
+                        out=w_planes[part][r:P:32].bitcast(I32),
+                        in_=scales_by_row[r:16:4, :, part * PART_COLS : (part + 1) * PART_COLS].bitcast(I32),
+                    )
 
         x_words = x_sb[:].bitcast(F32)
         for j in range(TOKEN_TILES):
@@ -110,8 +119,6 @@ def tile_jointattention_pa_kernel(tc, img, rope, w_words, w_scales, out_q, out_k
             turn = c % GROUPS_PER_PART
             rotated = part < 2
             stage = stages.tile([P, GROUP_HEADS, TOKEN_TILES, D], F32)
-            if rotated:
-                cross = crosses.tile([P, 2, GROUP_HEADS, TOKEN_TILES, PAIRS], F32)
             for j in range(TOKEN_TILES):
                 acc = psum.tile([P, GROUP_COLS], F32, tag="bank")
                 for g in range(PASSES):
@@ -120,28 +127,26 @@ def tile_jointattention_pa_kernel(tc, img, rope, w_words, w_scales, out_q, out_k
                         lhsT=x_codes[:, j * PASSES + g, :].bitcast(FP8X4),
                         lhsT_scale=x_scales[:, j * PASSES + g, :],
                         rhs=w_sb[:, c, g, :].bitcast(FP4X4),
-                        rhs_scale=w_planes[:, part, g, turn * GROUP_COLS : (turn + 1) * GROUP_COLS],
+                        rhs_scale=w_planes[part][:, g, turn * GROUP_COLS : (turn + 1) * GROUP_COLS],
                         start=(g == 0),
                         stop=(g == PASSES - 1),
                     )
                 if not rotated:
                     nc.scalar.copy(out=stage[:, :, j, :], in_=acc[:].rearrange("p (h d) -> p h d", d=D))
                     continue
-                y_pairs = acc[:].rearrange("p (h i e) -> p h i e", h=GROUP_HEADS, e=2)
-                rope_pairs = rope_sb[:, j, :].rearrange("p (i e) -> p i e", e=2)
-                cos = rope_pairs[:, :, 0:1].unsqueeze(1).to_broadcast([P, GROUP_HEADS, PAIRS, 2])
-                sin = rope_pairs[:, :, 1].unsqueeze(1).to_broadcast([P, GROUP_HEADS, PAIRS])
+                shape = [P, 2, GROUP_HEADS, PAIRS, 2]
+                product = products.tile([P, 2, GROUP_COLS], F32)
                 nc.vector.tensor_tensor(
-                    out=stage[:, :, j, :].rearrange("p h (i e) -> p h i e", e=2), in0=y_pairs, in1=cos, op=MULT
+                    out=product[:].rearrange("p e (h i f) -> p e h i f", h=GROUP_HEADS, f=2),
+                    in0=acc[:].rearrange("p (h i e) -> p e h i", h=GROUP_HEADS, e=2).unsqueeze(4).to_broadcast(shape),
+                    in1=table_pairs[:, j].unsqueeze(2).to_broadcast(shape),
+                    op=MULT,
                 )
-                nc.vector.scalar_tensor_tensor(
-                    out=cross[:, 0, :, j, :], in0=y_pairs[:, :, :, 1], scalar=-1.0, in1=sin, op0=MULT, op1=MULT
-                )
-                nc.vector.tensor_tensor(out=cross[:, 1, :, j, :], in0=y_pairs[:, :, :, 0], in1=sin, op=MULT)
-            if rotated:
-                stage_pairs = stage[:].rearrange("p h j (i e) -> p (h j i) e", e=2)
                 nc.gpsimd.tensor_tensor(
-                    out=stage_pairs, in0=stage_pairs, in1=cross[:].rearrange("p e h j i -> p (h j i) e"), op=ADD
+                    out=stage[:, :, j, :],
+                    in0=product[:, 0, :].rearrange("p (h d) -> p h d", d=D),
+                    in1=product[:, 1, :].rearrange("p (h d) -> p h d", d=D),
+                    op=ADD,
                 )
             heads = outs[part][0, turn * GROUP_HEADS : (turn + 1) * GROUP_HEADS]
             nc.sync.dma_start(

@@ -29,6 +29,8 @@ GROUP_HEADS = GROUP_COLS // D
 GROUPS_PER_PART = HEADS // GROUP_HEADS
 PART_COLS = HEADS * D
 
+WARM_UP = 6
+
 FLOPS = 2 * TOKENS * HID * PARTS * PART_COLS
 
 
@@ -59,6 +61,19 @@ def tile_jointattention_pa_kernel(tc, img, rope, w_words, w_scales, out_q, out_k
         for part in range(PARTS):
             planes = keep.tile([P, PASSES, PART_COLS], U8, align_bytes=64, name="planes%d" % part)
             w_planes.append(planes)
+
+        zeros = keep.tile([P, GROUP_COLS], BF16)
+        unused = keep.tile([P, 1], BF16)
+        nc.vector.memset(zeros[:], 0.0)
+        nc.scalar.copy(out=unused[:], in_=zeros[:, 0:1])
+        ctx.enter_context(tc.manual_schedule(engines={mybir.EngineType.PE}))
+        idle_bank = psum.tile([P, GROUP_COLS], F32, tag="bank")
+
+        def keep_tensor_busy(times):
+            for n in range(times):
+                nc.tensor.matmul(idle_bank[:], lhsT=zeros[:, 0:P], rhs=zeros[:], start=True, stop=True)
+
+        keep_tensor_busy(WARM_UP)
 
         for part in range(PARTS):
             nc.vector.memset(w_planes[part][:].bitcast(I32), 0)
@@ -113,6 +128,7 @@ def tile_jointattention_pa_kernel(tc, img, rope, w_words, w_scales, out_q, out_k
                     scales=x_scales[:, unit, :],
                     in_=grouped[:, unit, :],
                 )
+            keep_tensor_busy(1)
 
         for c in column_groups_in_turn():
             part = c // GROUPS_PER_PART

@@ -57,16 +57,20 @@ def tile_jointattention_pa_kernel(tc, img, rope, w_words, w_scales, out_q, out_k
         x_codes = keep.tile([P, TOKEN_TILES * PASSES, P], U32, align_bytes=64)
         x_scales = keep.tile([P, TOKEN_TILES * PASSES, P], U8, align_bytes=64)
         w_sb = keep.tile([P, PARTS * GROUPS_PER_PART, PASSES, 2 * GROUP_COLS], U8, align_bytes=64)
-        w_planes = []
+        first_planes = []
+        later_planes = []
         for part in range(PARTS):
-            planes = keep.tile([P, PASSES, PART_COLS], U8, align_bytes=64, name="planes%d" % part)
-            w_planes.append(planes)
+            planes = keep.tile([P, PASSES, GROUP_COLS], U8, align_bytes=64, name="first_planes%d" % part)
+            first_planes.append(planes)
+            planes = keep.tile([P, PASSES, PART_COLS - GROUP_COLS], U8, align_bytes=64, name="later_planes%d" % part)
+            later_planes.append(planes)
 
         zeros = keep.tile([P, GROUP_COLS], BF16)
         unused = keep.tile([P, 1], BF16)
+        nc.vector.memset(first_planes[0][:].bitcast(I32), 0)
         nc.vector.memset(zeros[:], 0.0)
         nc.scalar.copy(out=unused[:], in_=zeros[:, 0:1])
-        ctx.enter_context(tc.manual_schedule(engines={mybir.EngineType.PE}))
+        ctx.enter_context(tc.manual_schedule(engines={mybir.EngineType.PE, mybir.EngineType.SP}))
         idle_bank = psum.tile([P, GROUP_COLS], F32, tag="bank")
 
         def keep_tensor_busy(times):
@@ -75,13 +79,44 @@ def tile_jointattention_pa_kernel(tc, img, rope, w_words, w_scales, out_q, out_k
 
         keep_tensor_busy(WARM_UP)
 
-        for part in range(PARTS):
-            nc.vector.memset(w_planes[part][:].bitcast(I32), 0)
+        nc.vector.memset(later_planes[0][:].bitcast(I32), 0)
+        for part in (2, 1):
+            nc.vector.memset(first_planes[part][:].bitcast(I32), 0)
+            nc.vector.memset(later_planes[part][:].bitcast(I32), 0)
         make_identity(nc, ident[:])
 
         img_rows = img[0].rearrange("(p j) k -> p j k", j=TOKEN_TILES)
-        for j in range(TOKEN_TILES):
+        words_by_partition = w_words.rearrange("g p b -> p g b")
+        scales_by_row = w_scales.rearrange("g q n -> q g n")
+
+        def load_tokens(j):
             nc.sync.dma_start(out=x_sb[:, j, :], in_=img_rows[:, j, :])
+
+        def load_words(c):
+            nc.sync.dma_start(
+                out=w_sb[:, c].bitcast(I32),
+                in_=words_by_partition[:, :, c * 2 * GROUP_COLS : (c + 1) * 2 * GROUP_COLS].bitcast(I32),
+            )
+
+        def load_planes(planes, first_col, cols):
+            for r in range(4):
+                nc.sync.dma_start(
+                    out=planes[r:P:32].bitcast(I32),
+                    in_=scales_by_row[r:16:4, :, first_col : first_col + cols].bitcast(I32),
+                )
+
+        load_tokens(0)
+        for c in column_groups_in_turn():
+            part = c // GROUPS_PER_PART
+            turn = c % GROUPS_PER_PART
+            if turn == 0:
+                load_planes(first_planes[part], part * PART_COLS, GROUP_COLS)
+            if turn == 1:
+                load_planes(later_planes[part], part * PART_COLS + GROUP_COLS, PART_COLS - GROUP_COLS)
+            load_words(c)
+            if c == 0:
+                load_tokens(1)
+                load_tokens(2)
         nc.scalar.dma_start(out=table[:, :, 0, :], in_=rope[0].rearrange("(p j) d -> p j d", j=TOKEN_TILES))
         table_pairs = table[:].rearrange("p j e (i f) -> p j e i f", f=2)
         nc.gpsimd.tensor_scalar(
@@ -90,23 +125,6 @@ def tile_jointattention_pa_kernel(tc, img, rope, w_words, w_scales, out_q, out_k
         nc.gpsimd.tensor_scalar(
             out=table_pairs[:, :, 1, :, 1], in0=table_pairs[:, :, 0, :, 0], scalar1=1.0, scalar2=0.0, op0=MULT, op1=ADD
         )
-
-        words_by_partition = w_words.rearrange("g p b -> p g b")
-        scales_by_row = w_scales.rearrange("g q n -> q g n")
-        parts_loaded = []
-        for c in column_groups_in_turn():
-            part = c // GROUPS_PER_PART
-            nc.sync.dma_start(
-                out=w_sb[:, c].bitcast(I32),
-                in_=words_by_partition[:, :, c * 2 * GROUP_COLS : (c + 1) * 2 * GROUP_COLS].bitcast(I32),
-            )
-            if part not in parts_loaded:
-                parts_loaded.append(part)
-                for r in range(4):
-                    nc.sync.dma_start(
-                        out=w_planes[part][r:P:32].bitcast(I32),
-                        in_=scales_by_row[r:16:4, :, part * PART_COLS : (part + 1) * PART_COLS].bitcast(I32),
-                    )
 
         x_words = x_sb[:].bitcast(F32)
         for j in range(TOKEN_TILES):
@@ -135,6 +153,10 @@ def tile_jointattention_pa_kernel(tc, img, rope, w_words, w_scales, out_q, out_k
             turn = c % GROUPS_PER_PART
             rotated = part < 2
             stage = stages.tile([P, GROUP_HEADS, TOKEN_TILES, D], F32)
+            if turn == 0:
+                planes = first_planes[part][:]
+            else:
+                planes = later_planes[part][:, :, (turn - 1) * GROUP_COLS : turn * GROUP_COLS]
             for j in range(TOKEN_TILES):
                 acc = psum.tile([P, GROUP_COLS], F32, tag="bank")
                 for g in range(PASSES):
@@ -143,7 +165,7 @@ def tile_jointattention_pa_kernel(tc, img, rope, w_words, w_scales, out_q, out_k
                         lhsT=x_codes[:, j * PASSES + g, :].bitcast(FP8X4),
                         lhsT_scale=x_scales[:, j * PASSES + g, :],
                         rhs=w_sb[:, c, g, :].bitcast(FP4X4),
-                        rhs_scale=w_planes[part][:, g, turn * GROUP_COLS : (turn + 1) * GROUP_COLS],
+                        rhs_scale=planes[:, g, :],
                         start=(g == 0),
                         stop=(g == PASSES - 1),
                     )

@@ -34,11 +34,8 @@ WARM_UP = 6
 FLOPS = 2 * TOKENS * HID * PARTS * PART_COLS
 
 
-def column_groups_in_turn():
-    order = []
-    for turn in range(GROUPS_PER_PART):
-        order.extend([2 * turn, 2 * turn + 1, 2 * GROUPS_PER_PART + turn])
-    return order
+GROUP_ORDER = (0, 1, 2, 6, 3, 7, 4, 5, 8)
+LOADS = ((0, 1), (1, 3), (6, 9), (3, 6))
 
 
 def tile_jointattention_pa_kernel(tc, img, rope, w_words, w_scales, out_q, out_k, out_v):
@@ -56,18 +53,17 @@ def tile_jointattention_pa_kernel(tc, img, rope, w_words, w_scales, out_q, out_k
         grouped = keep.tile([P, TOKEN_TILES * PASSES, K_PASS], BF16, align_bytes=64)
         x_codes = keep.tile([P, TOKEN_TILES * PASSES, P], U32, align_bytes=64)
         x_scales = keep.tile([P, TOKEN_TILES * PASSES, P], U8, align_bytes=64)
-        w_sb = keep.tile([P, PARTS * GROUPS_PER_PART, PASSES, 2 * GROUP_COLS], U8, align_bytes=64)
-        first_planes = []
-        later_planes = []
-        for part in range(PARTS):
-            planes = keep.tile([P, PASSES, GROUP_COLS], U8, align_bytes=64, name="first_planes%d" % part)
-            first_planes.append(planes)
-            planes = keep.tile([P, PASSES, PART_COLS - GROUP_COLS], U8, align_bytes=64, name="later_planes%d" % part)
-            later_planes.append(planes)
+        w_words_sb = []
+        w_planes = []
+        for first, end in LOADS:
+            words = keep.tile([P, PASSES, (end - first) * 2 * GROUP_COLS], U8, align_bytes=64, name="words%d" % first)
+            w_words_sb.append(words)
+            planes = keep.tile([P, PASSES, (end - first) * GROUP_COLS], U8, align_bytes=64, name="planes%d" % first)
+            w_planes.append(planes)
 
         zeros = keep.tile([P, GROUP_COLS], BF16)
         unused = keep.tile([P, 1], BF16)
-        nc.vector.memset(first_planes[0][:].bitcast(I32), 0)
+        nc.vector.memset(w_planes[0][:].bitcast(I32), 0)
         nc.vector.memset(zeros[:], 0.0)
         nc.scalar.copy(out=unused[:], in_=zeros[:, 0:1])
         ctx.enter_context(tc.manual_schedule(engines={mybir.EngineType.PE, mybir.EngineType.SP}))
@@ -79,10 +75,8 @@ def tile_jointattention_pa_kernel(tc, img, rope, w_words, w_scales, out_q, out_k
 
         keep_tensor_busy(WARM_UP)
 
-        nc.vector.memset(later_planes[0][:].bitcast(I32), 0)
-        for part in (2, 1):
-            nc.vector.memset(first_planes[part][:].bitcast(I32), 0)
-            nc.vector.memset(later_planes[part][:].bitcast(I32), 0)
+        for planes in w_planes[1:]:
+            nc.vector.memset(planes[:].bitcast(I32), 0)
         make_identity(nc, ident[:])
 
         img_rows = img[0].rearrange("(p j) k -> p j k", j=TOKEN_TILES)
@@ -92,31 +86,24 @@ def tile_jointattention_pa_kernel(tc, img, rope, w_words, w_scales, out_q, out_k
         def load_tokens(j):
             nc.sync.dma_start(out=x_sb[:, j, :], in_=img_rows[:, j, :])
 
-        def load_words(c):
-            nc.sync.dma_start(
-                out=w_sb[:, c].bitcast(I32),
-                in_=words_by_partition[:, :, c * 2 * GROUP_COLS : (c + 1) * 2 * GROUP_COLS].bitcast(I32),
-            )
-
-        def load_planes(planes, first_col, cols):
+        def load_weights(n):
+            first, end = LOADS[n]
             for r in range(4):
                 nc.sync.dma_start(
-                    out=planes[r:P:32].bitcast(I32),
-                    in_=scales_by_row[r:16:4, :, first_col : first_col + cols].bitcast(I32),
+                    out=w_planes[n][r:P:32].bitcast(I32),
+                    in_=scales_by_row[r:16:4, :, first * GROUP_COLS : end * GROUP_COLS].bitcast(I32),
                 )
+            nc.sync.dma_start(
+                out=w_words_sb[n][:].bitcast(I32),
+                in_=words_by_partition[:, :, first * 2 * GROUP_COLS : end * 2 * GROUP_COLS].bitcast(I32),
+            )
 
         load_tokens(0)
-        for c in column_groups_in_turn():
-            part = c // GROUPS_PER_PART
-            turn = c % GROUPS_PER_PART
-            if turn == 0:
-                load_planes(first_planes[part], part * PART_COLS, GROUP_COLS)
-            if turn == 1:
-                load_planes(later_planes[part], part * PART_COLS + GROUP_COLS, PART_COLS - GROUP_COLS)
-            load_words(c)
-            if c == 0:
-                load_tokens(1)
-                load_tokens(2)
+        load_weights(0)
+        load_tokens(1)
+        load_tokens(2)
+        for n in range(1, len(LOADS)):
+            load_weights(n)
         nc.scalar.dma_start(out=table[:, :, 0, :], in_=rope[0].rearrange("(p j) d -> p j d", j=TOKEN_TILES))
         table_pairs = table[:].rearrange("p j e (i f) -> p j e i f", f=2)
         nc.gpsimd.tensor_scalar(
@@ -148,15 +135,15 @@ def tile_jointattention_pa_kernel(tc, img, rope, w_words, w_scales, out_q, out_k
                 )
             keep_tensor_busy(1)
 
-        for c in column_groups_in_turn():
+        for c in GROUP_ORDER:
             part = c // GROUPS_PER_PART
             turn = c % GROUPS_PER_PART
             rotated = part < 2
             stage = stages.tile([P, GROUP_HEADS, TOKEN_TILES, D], F32)
-            if turn == 0:
-                planes = first_planes[part][:]
-            else:
-                planes = later_planes[part][:, :, (turn - 1) * GROUP_COLS : turn * GROUP_COLS]
+            n = [first <= c < end for first, end in LOADS].index(True)
+            place = c - LOADS[n][0]
+            words = w_words_sb[n][:, :, place * 2 * GROUP_COLS : (place + 1) * 2 * GROUP_COLS]
+            planes = w_planes[n][:, :, place * GROUP_COLS : (place + 1) * GROUP_COLS]
             for j in range(TOKEN_TILES):
                 acc = psum.tile([P, GROUP_COLS], F32, tag="bank")
                 for g in range(PASSES):
@@ -164,7 +151,7 @@ def tile_jointattention_pa_kernel(tc, img, rope, w_words, w_scales, out_q, out_k
                         out=acc[:],
                         lhsT=x_codes[:, j * PASSES + g, :].bitcast(FP8X4),
                         lhsT_scale=x_scales[:, j * PASSES + g, :],
-                        rhs=w_sb[:, c, g, :].bitcast(FP4X4),
+                        rhs=words[:, g, :].bitcast(FP4X4),
                         rhs_scale=planes[:, g, :],
                         start=(g == 0),
                         stop=(g == PASSES - 1),

@@ -36,6 +36,7 @@ FLOPS = 2 * TOKENS * HID * PARTS * PART_COLS
 
 GROUP_ORDER = (0, 1, 2, 6, 3, 7, 4, 5, 8)
 LOADS = ((0, 1), (1, 3), (6, 9), (3, 6))
+VECTOR_ALONE = ((1, 2), (3, 2), (5, 2))
 
 
 def tile_jointattention_pa_kernel(tc, img, rope, w_words, w_scales, out_q, out_k, out_v):
@@ -49,6 +50,7 @@ def tile_jointattention_pa_kernel(tc, img, rope, w_words, w_scales, out_q, out_k
 
         x_sb = keep.tile([P, TOKEN_TILES, HID], BF16)
         table = keep.tile([P, TOKEN_TILES, 2, D], BF16)
+        table_alone = keep.tile([P, TOKEN_TILES, 2 * D], BF16)
         ident = keep.tile([P, P], F32)
         grouped = keep.tile([P, TOKEN_TILES * PASSES, K_PASS], BF16, align_bytes=64)
         x_codes = keep.tile([P, TOKEN_TILES * PASSES, P], U32, align_bytes=64)
@@ -113,6 +115,13 @@ def tile_jointattention_pa_kernel(tc, img, rope, w_words, w_scales, out_q, out_k
             out=table_pairs[:, :, 1, :, 1], in0=table_pairs[:, :, 0, :, 0], scalar1=1.0, scalar2=0.0, op0=MULT, op1=ADD
         )
 
+        alone_pairs = table_alone[:].rearrange("p j (i f e) -> p j i f e", f=2, e=2)
+        for e in range(2):
+            for f in range(2):
+                nc.gpsimd.tensor_scalar(
+                    out=alone_pairs[:, :, :, f, e], in0=table_pairs[:, :, e, :, f], scalar1=1.0, scalar2=0.0, op0=MULT, op1=ADD
+                )
+
         x_words = x_sb[:].bitcast(F32)
         for j in range(TOKEN_TILES):
             for g in range(PASSES):
@@ -159,8 +168,24 @@ def tile_jointattention_pa_kernel(tc, img, rope, w_words, w_scales, out_q, out_k
                 if not rotated:
                     nc.scalar.copy(out=stage[:, :, j, :], in_=acc[:].rearrange("p (h d) -> p h d", d=D))
                     continue
-                shape = [P, 2, GROUP_HEADS, PAIRS, 2]
                 product = products.tile([P, 2, GROUP_COLS], F32)
+                if (c, j) in VECTOR_ALONE:
+                    shape = [P, GROUP_HEADS, PAIRS, 2, 2]
+                    flat = product[:].rearrange("p e x -> p (e x)")
+                    nc.vector.tensor_tensor(
+                        out=flat.rearrange("p (h i f e) -> p h i f e", h=GROUP_HEADS, f=2, e=2),
+                        in0=acc[:].rearrange("p (h i e) -> p h i e", h=GROUP_HEADS, e=2).unsqueeze(3).to_broadcast(shape),
+                        in1=alone_pairs[:, j].unsqueeze(1).to_broadcast(shape),
+                        op=MULT,
+                    )
+                    nc.vector.tensor_reduce(
+                        out=stage[:, :, j, :],
+                        in_=flat.rearrange("p (h d e) -> p h d e", h=GROUP_HEADS, e=2),
+                        axis=mybir.AxisListType.X,
+                        op=ADD,
+                    )
+                    continue
+                shape = [P, 2, GROUP_HEADS, PAIRS, 2]
                 nc.vector.tensor_tensor(
                     out=product[:].rearrange("p e (h i f) -> p e h i f", h=GROUP_HEADS, f=2),
                     in0=acc[:].rearrange("p (h i e) -> p e h i", h=GROUP_HEADS, e=2).unsqueeze(4).to_broadcast(shape),

@@ -29,14 +29,15 @@ GROUP_HEADS = GROUP_COLS // D
 GROUPS_PER_PART = HEADS // GROUP_HEADS
 PART_COLS = HEADS * D
 
-WARM_UP = 6
+WARM_UP = 3
 
 FLOPS = 2 * TOKENS * HID * PARTS * PART_COLS
 
 
 GROUP_ORDER = (0, 1, 2, 6, 3, 7, 4, 5, 8)
 LOADS = ((0, 1), (1, 3), (6, 9), (3, 6))
-VECTOR_ALONE = ((1, 2), (3, 2), (5, 2))
+VECTOR_ALONE = ((2, 2), (5, 2))
+BY_HEAD = ()
 
 
 def tile_jointattention_pa_kernel(tc, img, rope, w_words, w_scales, out_q, out_k, out_v):
@@ -44,7 +45,7 @@ def tile_jointattention_pa_kernel(tc, img, rope, w_words, w_scales, out_q, out_k
     outs = (out_q, out_k, out_v)
     with ExitStack() as ctx:
         keep = ctx.enter_context(tc.tile_pool(name="keep", bufs=1))
-        stages = ctx.enter_context(tc.tile_pool(name="stages", bufs=4))
+        stages = ctx.enter_context(tc.tile_pool(name="stages", bufs=len(GROUP_ORDER)))
         products = ctx.enter_context(tc.tile_pool(name="products", bufs=4))
         psum = ctx.enter_context(tc.psum_pool(name="psum", bufs=8))
 
@@ -100,11 +101,9 @@ def tile_jointattention_pa_kernel(tc, img, rope, w_words, w_scales, out_q, out_k
                 in_=words_by_partition[:, :, first * 2 * GROUP_COLS : end * 2 * GROUP_COLS].bitcast(I32),
             )
 
-        load_tokens(0)
-        load_weights(0)
-        load_tokens(1)
-        load_tokens(2)
-        for n in range(1, len(LOADS)):
+        for j in range(TOKEN_TILES):
+            load_tokens(j)
+        for n in range(len(LOADS)):
             load_weights(n)
         nc.scalar.dma_start(out=table[:, :, 0, :], in_=rope[0].rearrange("(p j) d -> p j d", j=TOKEN_TILES))
         table_pairs = table[:].rearrange("p j e (i f) -> p j e i f", f=2)
@@ -123,7 +122,8 @@ def tile_jointattention_pa_kernel(tc, img, rope, w_words, w_scales, out_q, out_k
                 )
 
         x_words = x_sb[:].bitcast(F32)
-        for j in range(TOKEN_TILES):
+
+        def quantise_tokens(j):
             for g in range(PASSES):
                 unit = j * PASSES + g
                 flipped = psum.tile([P, GROUP_COLS], F32, tag="bank")
@@ -142,64 +142,116 @@ def tile_jointattention_pa_kernel(tc, img, rope, w_words, w_scales, out_q, out_k
                     scales=x_scales[:, unit, :],
                     in_=grouped[:, unit, :],
                 )
-            keep_tensor_busy(1)
 
-        for c in GROUP_ORDER:
+        def multiply(out, j, words, planes):
+            for g in range(PASSES):
+                nc.tensor.matmul_mx(
+                    out=out,
+                    lhsT=x_codes[:, j * PASSES + g, :].bitcast(FP8X4),
+                    lhsT_scale=x_scales[:, j * PASSES + g, :],
+                    rhs=words[:, g, :].bitcast(FP4X4),
+                    rhs_scale=planes[:, g, :],
+                    start=(g == 0),
+                    stop=(g == PASSES - 1),
+                )
+
+        def rotate(out, y, rows, factors, factors_alone, alone):
+            product = products.tile([P, 2, GROUP_COLS], F32)
+            if alone:
+                flat = product[:].rearrange("p e x -> p (e x)")[:, 0 : 2 * rows * D]
+                nc.vector.tensor_tensor(
+                    out=flat.rearrange("p (r i f e) -> p r i f e", r=rows, f=2, e=2),
+                    in0=y.rearrange("p (r i e) -> p r i e", r=rows, e=2).unsqueeze(3).to_broadcast([P, rows, PAIRS, 2, 2]),
+                    in1=factors_alone,
+                    op=MULT,
+                )
+                nc.vector.tensor_reduce(
+                    out=out, in_=flat.rearrange("p (r d e) -> p r d e", r=rows, e=2), axis=mybir.AxisListType.X, op=ADD
+                )
+                return
+            planes_of_product = product[:, :, 0 : rows * D]
+            nc.vector.tensor_tensor(
+                out=planes_of_product.rearrange("p e (r i f) -> p e r i f", r=rows, f=2),
+                in0=y.rearrange("p (r i e) -> p e r i", r=rows, e=2).unsqueeze(4).to_broadcast([P, 2, rows, PAIRS, 2]),
+                in1=factors,
+                op=MULT,
+            )
+            nc.gpsimd.tensor_tensor(
+                out=out,
+                in0=planes_of_product[:, 0, :].rearrange("p (r d) -> p r d", d=D),
+                in1=planes_of_product[:, 1, :].rearrange("p (r d) -> p r d", d=D),
+                op=ADD,
+            )
+
+        def open_group(c):
             part = c // GROUPS_PER_PART
             turn = c % GROUPS_PER_PART
-            rotated = part < 2
-            stage = stages.tile([P, GROUP_HEADS, TOKEN_TILES, D], F32)
             n = [first <= c < end for first, end in LOADS].index(True)
             place = c - LOADS[n][0]
             words = w_words_sb[n][:, :, place * 2 * GROUP_COLS : (place + 1) * 2 * GROUP_COLS]
             planes = w_planes[n][:, :, place * GROUP_COLS : (place + 1) * GROUP_COLS]
-            for j in range(TOKEN_TILES):
-                acc = psum.tile([P, GROUP_COLS], F32, tag="bank")
-                for g in range(PASSES):
-                    nc.tensor.matmul_mx(
-                        out=acc[:],
-                        lhsT=x_codes[:, j * PASSES + g, :].bitcast(FP8X4),
-                        lhsT_scale=x_scales[:, j * PASSES + g, :],
-                        rhs=words[:, g, :].bitcast(FP4X4),
-                        rhs_scale=planes[:, g, :],
-                        start=(g == 0),
-                        stop=(g == PASSES - 1),
-                    )
-                if not rotated:
-                    nc.scalar.copy(out=stage[:, :, j, :], in_=acc[:].rearrange("p (h d) -> p h d", d=D))
-                    continue
-                product = products.tile([P, 2, GROUP_COLS], F32)
-                if (c, j) in VECTOR_ALONE:
-                    shape = [P, GROUP_HEADS, PAIRS, 2, 2]
-                    flat = product[:].rearrange("p e x -> p (e x)")
-                    nc.vector.tensor_tensor(
-                        out=flat.rearrange("p (h i f e) -> p h i f e", h=GROUP_HEADS, f=2, e=2),
-                        in0=acc[:].rearrange("p (h i e) -> p h i e", h=GROUP_HEADS, e=2).unsqueeze(3).to_broadcast(shape),
-                        in1=alone_pairs[:, j].unsqueeze(1).to_broadcast(shape),
-                        op=MULT,
-                    )
-                    nc.vector.tensor_reduce(
-                        out=stage[:, :, j, :],
-                        in_=flat.rearrange("p (h d e) -> p h d e", h=GROUP_HEADS, e=2),
-                        axis=mybir.AxisListType.X,
-                        op=ADD,
-                    )
-                    continue
-                shape = [P, 2, GROUP_HEADS, PAIRS, 2]
-                nc.vector.tensor_tensor(
-                    out=product[:].rearrange("p e (h i f) -> p e h i f", h=GROUP_HEADS, f=2),
-                    in0=acc[:].rearrange("p (h i e) -> p e h i", h=GROUP_HEADS, e=2).unsqueeze(4).to_broadcast(shape),
-                    in1=table_pairs[:, j].unsqueeze(2).to_broadcast(shape),
-                    op=MULT,
-                )
-                nc.gpsimd.tensor_tensor(
-                    out=stage[:, :, j, :],
-                    in0=product[:, 0, :].rearrange("p (h d) -> p h d", d=D),
-                    in1=product[:, 1, :].rearrange("p (h d) -> p h d", d=D),
-                    op=ADD,
-                )
             heads = outs[part][0, turn * GROUP_HEADS : (turn + 1) * GROUP_HEADS]
-            nc.sync.dma_start(
-                out=heads.rearrange("h (p j) d -> p h (j d)", j=TOKEN_TILES),
-                in_=stage[:].rearrange("p h j d -> p h (j d)"),
-            )
+            runs = heads.rearrange("h (p j) d -> p h (j d)", j=TOKEN_TILES)
+            stage = stages.tile([P, GROUP_HEADS, TOKEN_TILES, D], F32, name="stage")
+            return words, planes, runs, stage
+
+        def bank_of_tile(c, j, group):
+            words, planes, runs, stage = group
+            acc = psum.tile([P, GROUP_COLS], F32, tag="bank")
+            multiply(acc[:], j, words, planes)
+            if c < 2 * GROUPS_PER_PART:
+                rotate(
+                    stage[:, :, j, :],
+                    acc[:],
+                    GROUP_HEADS,
+                    table_pairs[:, j].unsqueeze(2).to_broadcast([P, 2, GROUP_HEADS, PAIRS, 2]),
+                    alone_pairs[:, j].unsqueeze(1).to_broadcast([P, GROUP_HEADS, PAIRS, 2, 2]),
+                    (c, j) in VECTOR_ALONE,
+                )
+            else:
+                nc.scalar.copy(out=stage[:, :, j, :], in_=acc[:].rearrange("p (h d) -> p h d", d=D))
+
+        def store_group(group):
+            words, planes, runs, stage = group
+            nc.sync.dma_start(out=runs, in_=stage[:].rearrange("p h j d -> p h (j d)"))
+
+        def bank_of_head(c, h, group):
+            words, planes, runs, stage = group
+            acc = psum.tile([P, GROUP_COLS], F32, tag="bank")
+            for j in range(TOKEN_TILES):
+                multiply(
+                    acc[:, j * D : (j + 1) * D], j, words[:, :, h * 2 * D : (h + 1) * 2 * D], planes[:, :, h * D : (h + 1) * D]
+                )
+            y = acc[:, 0 : TOKEN_TILES * D]
+            if c < 2 * GROUPS_PER_PART:
+                rotate(
+                    stage[:, h, :, :],
+                    y,
+                    TOKEN_TILES,
+                    table_pairs.rearrange("p j e i f -> p e j i f"),
+                    alone_pairs,
+                    (c, h) in VECTOR_ALONE,
+                )
+                nc.sync.dma_start(out=runs[:, h, :], in_=stage[:, h, :, :].rearrange("p j d -> p (j d)"))
+            else:
+                nc.scalar.copy(out=stage[:, h, :, :].rearrange("p j d -> p (j d)"), in_=y)
+                nc.scalar.dma_start(out=runs[:, h, :], in_=stage[:, h, :, :].rearrange("p j d -> p (j d)"))
+
+        for j in range(TOKEN_TILES):
+            quantise_tokens(j)
+            keep_tensor_busy(1)
+        held = []
+        for c in GROUP_ORDER[0:]:
+            group = open_group(c)
+            if c in BY_HEAD:
+                for h in range(GROUP_HEADS):
+                    bank_of_head(c, h, group)
+                continue
+            for j in range(TOKEN_TILES):
+                bank_of_tile(c, j, group)
+            if c == GROUP_ORDER[-2]:
+                held.append(group)
+            else:
+                store_group(group)
+        for group in held:
+            store_group(group)

@@ -29,7 +29,7 @@ GROUP_HEADS = GROUP_COLS // D
 GROUPS_PER_PART = HEADS // GROUP_HEADS
 PART_COLS = HEADS * D
 
-WARM_UP = 3
+WARM_UP = 5
 
 FLOPS = 2 * TOKENS * HID * PARTS * PART_COLS
 
@@ -67,7 +67,7 @@ def tile_jointattention_pa_kernel(tc, img, rope, w_words, w_scales, out_q, out_k
         zeros = keep.tile([P, GROUP_COLS], BF16)
         unused = keep.tile([P, 1], BF16)
         nc.vector.memset(w_planes[0][:].bitcast(I32), 0)
-        nc.vector.memset(zeros[:], 0.0)
+        nc.gpsimd.memset(zeros[:], 0.0)
         nc.scalar.copy(out=unused[:], in_=zeros[:, 0:1])
         ctx.enter_context(tc.manual_schedule(engines={mybir.EngineType.PE, mybir.EngineType.SP}))
         idle_bank = psum.tile([P, GROUP_COLS], F32, tag="bank")
@@ -89,22 +89,29 @@ def tile_jointattention_pa_kernel(tc, img, rope, w_words, w_scales, out_q, out_k
         def load_tokens(j):
             nc.sync.dma_start(out=x_sb[:, j, :], in_=img_rows[:, j, :])
 
-        def load_weights(n):
+        def load_planes(n):
             first, end = LOADS[n]
             for r in range(4):
                 nc.sync.dma_start(
                     out=w_planes[n][r:P:32].bitcast(I32),
                     in_=scales_by_row[r:16:4, :, first * GROUP_COLS : end * GROUP_COLS].bitcast(I32),
                 )
+
+        def load_words(n):
+            first, end = LOADS[n]
             nc.sync.dma_start(
                 out=w_words_sb[n][:].bitcast(I32),
                 in_=words_by_partition[:, :, first * 2 * GROUP_COLS : end * 2 * GROUP_COLS].bitcast(I32),
             )
 
-        for j in range(TOKEN_TILES):
-            load_tokens(j)
-        for n in range(len(LOADS)):
-            load_weights(n)
+        load_tokens(0)
+        load_planes(0)
+        load_tokens(1)
+        load_tokens(2)
+        load_words(0)
+        for n in range(1, len(LOADS)):
+            load_planes(n)
+            load_words(n)
         nc.scalar.dma_start(out=table[:, :, 0, :], in_=rope[0].rearrange("(p j) d -> p j d", j=TOKEN_TILES))
         table_pairs = table[:].rearrange("p j e (i f) -> p j e i f", f=2)
         nc.gpsimd.tensor_scalar(
@@ -239,7 +246,7 @@ def tile_jointattention_pa_kernel(tc, img, rope, w_words, w_scales, out_q, out_k
 
         for j in range(TOKEN_TILES):
             quantise_tokens(j)
-            keep_tensor_busy(1)
+            keep_tensor_busy(2 if j == 0 else 1)
         held = []
         for c in GROUP_ORDER[0:]:
             group = open_group(c)

@@ -35,7 +35,8 @@ FLOPS = 2 * TOKENS * HID * PARTS * PART_COLS
 
 
 GROUP_ORDER = (0, 1, 2, 6, 3, 7, 4, 5, 8)
-LOADS = ((0, 1), (1, 3), (6, 9), (3, 6))
+LOADS = ((0, 1), (1, 3), (6, 7), (3, 4), (7, 9), (4, 6))
+PLANE_LOADS = ((0, 1), (1, 3), (6, 9), (3, 6))
 VECTOR_ALONE = ((2, 2), (5, 2))
 BY_HEAD = ()
 
@@ -61,6 +62,7 @@ def tile_jointattention_pa_kernel(tc, img, rope, w_words, w_scales, out_q, out_k
         for first, end in LOADS:
             words = keep.tile([P, PASSES, (end - first) * 2 * GROUP_COLS], U8, align_bytes=64, name="words%d" % first)
             w_words_sb.append(words)
+        for first, end in PLANE_LOADS:
             planes = keep.tile([P, PASSES, (end - first) * GROUP_COLS], U8, align_bytes=64, name="planes%d" % first)
             w_planes.append(planes)
 
@@ -90,7 +92,7 @@ def tile_jointattention_pa_kernel(tc, img, rope, w_words, w_scales, out_q, out_k
             nc.sync.dma_start(out=x_sb[:, j, :], in_=img_rows[:, j, :])
 
         def load_planes(n):
-            first, end = LOADS[n]
+            first, end = PLANE_LOADS[n]
             for r in range(4):
                 nc.sync.dma_start(
                     out=w_planes[n][r:P:32].bitcast(I32),
@@ -110,7 +112,8 @@ def tile_jointattention_pa_kernel(tc, img, rope, w_words, w_scales, out_q, out_k
         load_tokens(2)
         load_words(0)
         for n in range(1, len(LOADS)):
-            load_planes(n)
+            if n < len(PLANE_LOADS):
+                load_planes(n)
             load_words(n)
         nc.scalar.dma_start(out=table[:, :, 0, :], in_=rope[0].rearrange("(p j) d -> p j d", j=TOKEN_TILES))
         table_pairs = table[:].rearrange("p j e (i f) -> p j e i f", f=2)
@@ -196,7 +199,9 @@ def tile_jointattention_pa_kernel(tc, img, rope, w_words, w_scales, out_q, out_k
             n = [first <= c < end for first, end in LOADS].index(True)
             place = c - LOADS[n][0]
             words = w_words_sb[n][:, :, place * 2 * GROUP_COLS : (place + 1) * 2 * GROUP_COLS]
-            planes = w_planes[n][:, :, place * GROUP_COLS : (place + 1) * GROUP_COLS]
+            m = [first <= c < end for first, end in PLANE_LOADS].index(True)
+            place = c - PLANE_LOADS[m][0]
+            planes = w_planes[m][:, :, place * GROUP_COLS : (place + 1) * GROUP_COLS]
             heads = outs[part][0, turn * GROUP_HEADS : (turn + 1) * GROUP_HEADS]
             runs = heads.rearrange("h (p j) d -> p h (j d)", j=TOKEN_TILES)
             stage = stages.tile([P, GROUP_HEADS, TOKEN_TILES, D], F32, name="stage")

@@ -51,6 +51,7 @@ def tile_jointattention_pa_kernel(tc, img, rope, w_words, w_scales, out_q, out_k
         psum = ctx.enter_context(tc.psum_pool(name="psum", bufs=8))
 
         x_sb = keep.tile([P, TOKEN_TILES, HID], BF16)
+        rope_rows = keep.tile([P, TOKEN_TILES, D], BF16)
         table = keep.tile([P, TOKEN_TILES, 2, D], BF16)
         table_alone = keep.tile([P, TOKEN_TILES, 2 * D], BF16)
         ident = keep.tile([P, P], F32)
@@ -115,21 +116,24 @@ def tile_jointattention_pa_kernel(tc, img, rope, w_words, w_scales, out_q, out_k
             if n < len(PLANE_LOADS):
                 load_planes(n)
             load_words(n)
-        nc.scalar.dma_start(out=table[:, :, 0, :], in_=rope[0].rearrange("(p j) d -> p j d", j=TOKEN_TILES))
+        nc.scalar.dma_start(out=rope_rows[:], in_=rope[0].rearrange("(p j) d -> p j d", j=TOKEN_TILES))
+        rope_pairs = rope_rows[:].rearrange("p j (i f) -> p j i f", f=2)
+        cosines = rope_pairs[:, :, :, 0]
+        sines = rope_pairs[:, :, :, 1]
         table_pairs = table[:].rearrange("p j e (i f) -> p j e i f", f=2)
-        nc.gpsimd.tensor_scalar(
-            out=table_pairs[:, :, 1, :, 0], in0=table_pairs[:, :, 0, :, 1], scalar1=-1.0, scalar2=0.0, op0=MULT, op1=ADD
-        )
-        nc.gpsimd.tensor_scalar(
-            out=table_pairs[:, :, 1, :, 1], in0=table_pairs[:, :, 0, :, 0], scalar1=1.0, scalar2=0.0, op0=MULT, op1=ADD
-        )
+
+        def factor(out, in_, sign):
+            nc.gpsimd.tensor_scalar(out=out, in0=in_, scalar1=sign, scalar2=0.0, op0=MULT, op1=ADD)
+
+        for f in range(2):
+            factor(table_pairs[:, :, 0, :, f], cosines, 1.0)
+            factor(table_pairs[:, :, 1, :, f], sines, 1.0 - 2.0 * f)
 
         alone_pairs = table_alone[:].rearrange("p j (i f e) -> p j i f e", f=2, e=2)
-        for e in range(2):
-            for f in range(2):
-                nc.gpsimd.tensor_scalar(
-                    out=alone_pairs[:, :, :, f, e], in0=table_pairs[:, :, e, :, f], scalar1=1.0, scalar2=0.0, op0=MULT, op1=ADD
-                )
+        factor(alone_pairs[:, :, :, 0, 0], cosines, 1.0)
+        factor(alone_pairs[:, :, :, 0, 1], sines, -1.0)
+        factor(alone_pairs[:, :, :, 1, 0], sines, 1.0)
+        factor(alone_pairs[:, :, :, 1, 1], cosines, 1.0)
 
         x_words = x_sb[:].bitcast(F32)
 
@@ -182,14 +186,14 @@ def tile_jointattention_pa_kernel(tc, img, rope, w_words, w_scales, out_q, out_k
             planes_of_product = product[:, :, 0 : rows * D]
             nc.vector.tensor_tensor(
                 out=planes_of_product.rearrange("p e (r i f) -> p e r i f", r=rows, f=2),
-                in0=y.rearrange("p (r i e) -> p e r i", r=rows, e=2).unsqueeze(4).to_broadcast([P, 2, rows, PAIRS, 2]),
+                in0=y.rearrange("p (r i f) -> p r i f", r=rows, f=2).unsqueeze(1).to_broadcast([P, 2, rows, PAIRS, 2]),
                 in1=factors,
                 op=MULT,
             )
             nc.gpsimd.tensor_tensor(
-                out=out,
-                in0=planes_of_product[:, 0, :].rearrange("p (r d) -> p r d", d=D),
-                in1=planes_of_product[:, 1, :].rearrange("p (r d) -> p r d", d=D),
+                out=out.rearrange("p r (i f) -> p r i f", f=2),
+                in0=planes_of_product[:, 0, :].rearrange("p (r i f) -> p r i f", r=rows, f=2),
+                in1=planes_of_product[:, 1, :].rearrange("p (r i f) -> p r i f", r=rows, f=2)[:, :, :, ::-1],
                 op=ADD,
             )
 

@@ -38,7 +38,6 @@ GROUP_ORDER = (0, 1, 2, 6, 3, 7, 4, 5, 8)
 LOADS = ((0, 1), (1, 3), (6, 7), (3, 4), (7, 9), (4, 6))
 PLANE_LOADS = ((0, 1), (1, 3), (6, 9), (3, 6))
 VECTOR_ALONE = ((2, 2), (5, 2))
-BY_HEAD = ()
 
 
 def tile_jointattention_pa_kernel(tc, img, rope, w_words, w_scales, out_q, out_k, out_v):
@@ -169,31 +168,31 @@ def tile_jointattention_pa_kernel(tc, img, rope, w_words, w_scales, out_q, out_k
                     stop=(g == PASSES - 1),
                 )
 
-        def rotate(out, y, rows, factors, factors_alone, alone):
-            product = products.tile([P, 2, GROUP_COLS], F32)
-            if alone:
-                flat = product[:].rearrange("p e x -> p (e x)")[:, 0 : 2 * rows * D]
-                nc.vector.tensor_tensor(
-                    out=flat.rearrange("p (r i f e) -> p r i f e", r=rows, f=2, e=2),
-                    in0=y.rearrange("p (r i e) -> p r i e", r=rows, e=2).unsqueeze(3).to_broadcast([P, rows, PAIRS, 2, 2]),
-                    in1=factors_alone,
-                    op=MULT,
-                )
-                nc.vector.tensor_reduce(
-                    out=out, in_=flat.rearrange("p (r d e) -> p r d e", r=rows, e=2), axis=mybir.AxisListType.X, op=ADD
-                )
-                return
-            planes_of_product = product[:, :, 0 : rows * D]
+        def rotate_alone(out, y, j):
+            product = products.tile([P, 2 * GROUP_COLS], F32, name="product")
             nc.vector.tensor_tensor(
-                out=planes_of_product.rearrange("p e (r i f) -> p e r i f", r=rows, f=2),
-                in0=y.rearrange("p (r i f) -> p r i f", r=rows, f=2).unsqueeze(1).to_broadcast([P, 2, rows, PAIRS, 2]),
-                in1=factors,
+                out=product[:].rearrange("p (h i f e) -> p h i f e", h=GROUP_HEADS, f=2, e=2),
+                in0=y.rearrange("p (h i e) -> p h i e", h=GROUP_HEADS, e=2).unsqueeze(3).to_broadcast([P, GROUP_HEADS, PAIRS, 2, 2]),
+                in1=alone_pairs[:, j].unsqueeze(1).to_broadcast([P, GROUP_HEADS, PAIRS, 2, 2]),
                 op=MULT,
             )
+            nc.vector.tensor_reduce(
+                out=out, in_=product[:].rearrange("p (h d e) -> p h d e", h=GROUP_HEADS, e=2), axis=mybir.AxisListType.X, op=ADD
+            )
+
+        def multiply_by_table(product, y, j):
+            nc.vector.tensor_tensor(
+                out=product.rearrange("p e (h i f) -> p e h i f", h=GROUP_HEADS, f=2),
+                in0=y.rearrange("p (h i f) -> p h i f", h=GROUP_HEADS, f=2).unsqueeze(1).to_broadcast([P, 2, GROUP_HEADS, PAIRS, 2]),
+                in1=table_pairs[:, j].unsqueeze(2).to_broadcast([P, 2, GROUP_HEADS, PAIRS, 2]),
+                op=MULT,
+            )
+
+        def add_products(out, product):
             nc.gpsimd.tensor_tensor(
-                out=out.rearrange("p r (i f) -> p r i f", f=2),
-                in0=planes_of_product[:, 0, :].rearrange("p (r i f) -> p r i f", r=rows, f=2),
-                in1=planes_of_product[:, 1, :].rearrange("p (r i f) -> p r i f", r=rows, f=2)[:, :, :, ::-1],
+                out=out,
+                in0=product[:, 0, :].rearrange("p (h d) -> p h d", d=D),
+                in1=product[:, 1, :].rearrange("p (x f) -> p x f", f=2)[:, :, ::-1],
                 op=ADD,
             )
 
@@ -215,43 +214,18 @@ def tile_jointattention_pa_kernel(tc, img, rope, w_words, w_scales, out_q, out_k
             words, planes, runs, stage = group
             acc = psum.tile([P, GROUP_COLS], F32, tag="bank")
             multiply(acc[:], j, words, planes)
-            if c < 2 * GROUPS_PER_PART:
-                rotate(
-                    stage[:, :, j, :],
-                    acc[:],
-                    GROUP_HEADS,
-                    table_pairs[:, j].unsqueeze(2).to_broadcast([P, 2, GROUP_HEADS, PAIRS, 2]),
-                    alone_pairs[:, j].unsqueeze(1).to_broadcast([P, GROUP_HEADS, PAIRS, 2, 2]),
-                    (c, j) in VECTOR_ALONE,
-                )
-            else:
+            if c >= 2 * GROUPS_PER_PART:
                 nc.scalar.copy(out=stage[:, :, j, :], in_=acc[:].rearrange("p (h d) -> p h d", d=D))
+            elif (c, j) in VECTOR_ALONE:
+                rotate_alone(stage[:, :, j, :], acc[:], j)
+            else:
+                product = products.tile([P, 2, GROUP_COLS], F32, name="product")
+                multiply_by_table(product[:], acc[:], j)
+                add_products(stage[:, :, j, :], product[:])
 
         def store_group(group):
             words, planes, runs, stage = group
             nc.sync.dma_start(out=runs, in_=stage[:].rearrange("p h j d -> p h (j d)"))
-
-        def bank_of_head(c, h, group):
-            words, planes, runs, stage = group
-            acc = psum.tile([P, GROUP_COLS], F32, tag="bank")
-            for j in range(TOKEN_TILES):
-                multiply(
-                    acc[:, j * D : (j + 1) * D], j, words[:, :, h * 2 * D : (h + 1) * 2 * D], planes[:, :, h * D : (h + 1) * D]
-                )
-            y = acc[:, 0 : TOKEN_TILES * D]
-            if c < 2 * GROUPS_PER_PART:
-                rotate(
-                    stage[:, h, :, :],
-                    y,
-                    TOKEN_TILES,
-                    table_pairs.rearrange("p j e i f -> p e j i f"),
-                    alone_pairs,
-                    (c, h) in VECTOR_ALONE,
-                )
-                nc.sync.dma_start(out=runs[:, h, :], in_=stage[:, h, :, :].rearrange("p j d -> p (j d)"))
-            else:
-                nc.scalar.copy(out=stage[:, h, :, :].rearrange("p j d -> p (j d)"), in_=y)
-                nc.scalar.dma_start(out=runs[:, h, :], in_=stage[:, h, :, :].rearrange("p j d -> p (j d)"))
 
         for j in range(TOKEN_TILES):
             quantise_tokens(j)
@@ -259,10 +233,6 @@ def tile_jointattention_pa_kernel(tc, img, rope, w_words, w_scales, out_q, out_k
         held = []
         for c in GROUP_ORDER[0:]:
             group = open_group(c)
-            if c in BY_HEAD:
-                for h in range(GROUP_HEADS):
-                    bank_of_head(c, h, group)
-                continue
             for j in range(TOKEN_TILES):
                 bank_of_tile(c, j, group)
             if c == GROUP_ORDER[-2]:

@@ -36,6 +36,8 @@ FLOPS = 2 * TOKENS * HID * PARTS * PART_COLS
 
 GROUP_ORDER = (0, 1, 2, 6, 3, 7, 4, 5, 8)
 LOADS = ((0, 1), (1, 3), (6, 7), (3, 4), (7, 9), (4, 6))
+STORE_ORDER = (0, 1, 6, 2, 7, 3, 4, 8, 5)
+FIRST_HALVES = 2
 PLANE_LOADS = ((0, 1), (1, 3), (6, 9), (3, 6))
 VECTOR_ALONE = ((2, 2), (5, 2))
 
@@ -180,11 +182,11 @@ def tile_jointattention_pa_kernel(tc, img, rope, w_words, w_scales, out_q, out_k
                 out=out, in_=product[:].rearrange("p (h d e) -> p h d e", h=GROUP_HEADS, e=2), axis=mybir.AxisListType.X, op=ADD
             )
 
-        def multiply_by_table(product, y, j):
+        def multiply_by_table(product, y, j, heads):
             nc.vector.tensor_tensor(
-                out=product.rearrange("p e (h i f) -> p e h i f", h=GROUP_HEADS, f=2),
-                in0=y.rearrange("p (h i f) -> p h i f", h=GROUP_HEADS, f=2).unsqueeze(1).to_broadcast([P, 2, GROUP_HEADS, PAIRS, 2]),
-                in1=table_pairs[:, j].unsqueeze(2).to_broadcast([P, 2, GROUP_HEADS, PAIRS, 2]),
+                out=product.rearrange("p e (h i f) -> p e h i f", h=heads, f=2),
+                in0=y.rearrange("p (h i f) -> p h i f", h=heads, f=2).unsqueeze(1).to_broadcast([P, 2, heads, PAIRS, 2]),
+                in1=table_pairs[:, j].unsqueeze(2).to_broadcast([P, 2, heads, PAIRS, 2]),
                 op=MULT,
             )
 
@@ -212,6 +214,19 @@ def tile_jointattention_pa_kernel(tc, img, rope, w_words, w_scales, out_q, out_k
 
         def bank_of_tile(c, j, group):
             words, planes, runs, stage = group
+            if (c, j) == (GROUP_ORDER[0], 0):
+                heads = GROUP_HEADS // FIRST_HALVES
+                for half in range(FIRST_HALVES):
+                    acc = psum.tile([P, GROUP_COLS], F32, tag="bank")
+                    for n in range(heads):
+                        h = half * heads + n
+                        multiply(
+                            acc[:, n * D : (n + 1) * D], j, words[:, :, h * 2 * D : (h + 1) * 2 * D], planes[:, :, h * D : (h + 1) * D]
+                        )
+                    product = products.tile([P, 2, heads * D], F32, name="product")
+                    multiply_by_table(product[:], acc[:, 0 : heads * D], j, heads)
+                    add_products(stage[:, half * heads : (half + 1) * heads, j, :], product[:])
+                return
             acc = psum.tile([P, GROUP_COLS], F32, tag="bank")
             multiply(acc[:], j, words, planes)
             if c >= 2 * GROUPS_PER_PART:
@@ -220,7 +235,7 @@ def tile_jointattention_pa_kernel(tc, img, rope, w_words, w_scales, out_q, out_k
                 rotate_alone(stage[:, :, j, :], acc[:], j)
             else:
                 product = products.tile([P, 2, GROUP_COLS], F32, name="product")
-                multiply_by_table(product[:], acc[:], j)
+                multiply_by_table(product[:], acc[:], j, GROUP_HEADS)
                 add_products(stage[:, :, j, :], product[:])
 
         def store_group(group):
@@ -229,15 +244,13 @@ def tile_jointattention_pa_kernel(tc, img, rope, w_words, w_scales, out_q, out_k
 
         for j in range(TOKEN_TILES):
             quantise_tokens(j)
-            keep_tensor_busy(2 if j == 0 else 1)
-        held = []
-        for c in GROUP_ORDER[0:]:
-            group = open_group(c)
+            keep_tensor_busy(1 if j == 1 else 2)
+        computed = {}
+        stored = 0
+        for c in GROUP_ORDER:
+            computed[c] = open_group(c)
             for j in range(TOKEN_TILES):
-                bank_of_tile(c, j, group)
-            if c == GROUP_ORDER[-2]:
-                held.append(group)
-            else:
-                store_group(group)
-        for group in held:
-            store_group(group)
+                bank_of_tile(c, j, computed[c])
+            while stored < len(STORE_ORDER) and STORE_ORDER[stored] in computed:
+                store_group(computed[STORE_ORDER[stored]])
+                stored += 1

from contextlib import ExitStack

import concourse.mybir as mybir
from concourse.masks import make_identity

F32 = mybir.dt.float32
BF16 = mybir.dt.bfloat16
I32 = mybir.dt.int32
U32 = mybir.dt.uint32
U8 = mybir.dt.uint8
FP8X4 = mybir.dt.float8_e4m3fn_x4
FP4X4 = mybir.dt.float4_e2m1fn_x4
MULT = mybir.AluOpType.mult
ADD = mybir.AluOpType.add

P = 128
TOKENS = 384
HID = 1536
HEADS = 12
D = 128
PAIRS = D // 2
PARTS = 3

K_PASS = 512
PASSES = HID // K_PASS
TOKEN_TILES = TOKENS // P
GROUP_COLS = 512
GROUP_HEADS = GROUP_COLS // D
GROUPS_PER_PART = HEADS // GROUP_HEADS
PART_COLS = HEADS * D

WARM_UP = 5

FLOPS = 2 * TOKENS * HID * PARTS * PART_COLS


GROUP_ORDER = (0, 1, 2, 6, 3, 7, 4, 5, 8)
LOADS = ((0, 1), (1, 3), (6, 7), (3, 4), (7, 9), (4, 6))
STORE_ORDER = (0, 1, 6, 2, 7, 3, 4, 8, 5)
FIRST_HALVES = 2
PLANE_LOADS = ((0, 1), (1, 3), (6, 9), (3, 6))
VECTOR_ALONE = ((2, 2), (5, 2))


def tile_jointattention_pa_kernel(tc, img, rope, w_words, w_scales, out_q, out_k, out_v):
    nc = tc.nc
    outs = (out_q, out_k, out_v)
    with ExitStack() as ctx:
        keep = ctx.enter_context(tc.tile_pool(name="keep", bufs=1))
        stages = ctx.enter_context(tc.tile_pool(name="stages", bufs=len(GROUP_ORDER)))
        products = ctx.enter_context(tc.tile_pool(name="products", bufs=4))
        psum = ctx.enter_context(tc.psum_pool(name="psum", bufs=8))

        x_sb = keep.tile([P, TOKEN_TILES, HID], BF16)
        rope_rows = keep.tile([P, TOKEN_TILES, D], BF16)
        table = keep.tile([P, TOKEN_TILES, 2, D], BF16)
        table_alone = keep.tile([P, TOKEN_TILES, 2 * D], BF16)
        ident = keep.tile([P, P], F32)
        grouped = keep.tile([P, TOKEN_TILES * PASSES, K_PASS], BF16, align_bytes=64)
        x_codes = keep.tile([P, TOKEN_TILES * PASSES, P], U32, align_bytes=64)
        x_scales = keep.tile([P, TOKEN_TILES * PASSES, P], U8, align_bytes=64)
        w_words_sb = []
        w_planes = []
        for first, end in LOADS:
            words = keep.tile([P, PASSES, (end - first) * 2 * GROUP_COLS], U8, align_bytes=64, name="words%d" % first)
            w_words_sb.append(words)
        for first, end in PLANE_LOADS:
            planes = keep.tile([P, PASSES, (end - first) * GROUP_COLS], U8, align_bytes=64, name="planes%d" % first)
            w_planes.append(planes)

        zeros = keep.tile([P, GROUP_COLS], BF16)
        unused = keep.tile([P, 1], BF16)
        nc.vector.memset(w_planes[0][:].bitcast(I32), 0)
        nc.gpsimd.memset(zeros[:], 0.0)
        nc.scalar.copy(out=unused[:], in_=zeros[:, 0:1])
        ctx.enter_context(tc.manual_schedule(engines={mybir.EngineType.PE, mybir.EngineType.SP}))
        idle_bank = psum.tile([P, GROUP_COLS], F32, tag="bank")

        def keep_tensor_busy(times):
            for n in range(times):
                nc.tensor.matmul(idle_bank[:], lhsT=zeros[:, 0:P], rhs=zeros[:], start=True, stop=True)

        keep_tensor_busy(WARM_UP)

        for planes in w_planes[1:]:
            nc.vector.memset(planes[:].bitcast(I32), 0)
        make_identity(nc, ident[:])

        img_rows = img[0].rearrange("(p j) k -> p j k", j=TOKEN_TILES)
        words_by_partition = w_words.rearrange("g p b -> p g b")
        scales_by_row = w_scales.rearrange("g q n -> q g n")

        def load_tokens(j):
            nc.sync.dma_start(out=x_sb[:, j, :], in_=img_rows[:, j, :])

        def load_planes(n):
            first, end = PLANE_LOADS[n]
            for r in range(4):
                nc.sync.dma_start(
                    out=w_planes[n][r:P:32].bitcast(I32),
                    in_=scales_by_row[r:16:4, :, first * GROUP_COLS : end * GROUP_COLS].bitcast(I32),
                )

        def load_words(n):
            first, end = LOADS[n]
            nc.sync.dma_start(
                out=w_words_sb[n][:].bitcast(I32),
                in_=words_by_partition[:, :, first * 2 * GROUP_COLS : end * 2 * GROUP_COLS].bitcast(I32),
            )

        load_tokens(0)
        load_planes(0)
        load_tokens(1)
        load_tokens(2)
        load_words(0)
        for n in range(1, len(LOADS)):
            if n < len(PLANE_LOADS):
                load_planes(n)
            load_words(n)
        nc.scalar.dma_start(out=rope_rows[:], in_=rope[0].rearrange("(p j) d -> p j d", j=TOKEN_TILES))
        rope_pairs = rope_rows[:].rearrange("p j (i f) -> p j i f", f=2)
        cosines = rope_pairs[:, :, :, 0]
        sines = rope_pairs[:, :, :, 1]
        table_pairs = table[:].rearrange("p j e (i f) -> p j e i f", f=2)

        def factor(out, in_, sign):
            nc.gpsimd.tensor_scalar(out=out, in0=in_, scalar1=sign, scalar2=0.0, op0=MULT, op1=ADD)

        for f in range(2):
            factor(table_pairs[:, :, 0, :, f], cosines, 1.0)
            factor(table_pairs[:, :, 1, :, f], sines, 1.0 - 2.0 * f)

        alone_pairs = table_alone[:].rearrange("p j (i f e) -> p j i f e", f=2, e=2)
        factor(alone_pairs[:, :, :, 0, 0], cosines, 1.0)
        factor(alone_pairs[:, :, :, 0, 1], sines, -1.0)
        factor(alone_pairs[:, :, :, 1, 0], sines, 1.0)
        factor(alone_pairs[:, :, :, 1, 1], cosines, 1.0)

        x_words = x_sb[:].bitcast(F32)

        def quantise_tokens(j):
            for g in range(PASSES):
                unit = j * PASSES + g
                flipped = psum.tile([P, GROUP_COLS], F32, tag="bank")
                for u in range(2):
                    nc.tensor.transpose(
                        flipped[:, u * P : (u + 1) * P],
                        x_words[:, j, 256 * g + u : 256 * (g + 1) : 2],
                        ident[:],
                    )
                nc.scalar.copy(
                    out=grouped[:, unit, :].bitcast(F32).rearrange("p (r u) -> p r u", u=2),
                    in_=flipped[:, 0 : 2 * P].rearrange("p (u r) -> p r u", u=2),
                )
                nc.vector.quantize_mx(
                    out=x_codes[:, unit, :].bitcast(FP8X4),
                    scales=x_scales[:, unit, :],
                    in_=grouped[:, unit, :],
                )

        def multiply(out, j, words, planes):
            for g in range(PASSES):
                nc.tensor.matmul_mx(
                    out=out,
                    lhsT=x_codes[:, j * PASSES + g, :].bitcast(FP8X4),
                    lhsT_scale=x_scales[:, j * PASSES + g, :],
                    rhs=words[:, g, :].bitcast(FP4X4),
                    rhs_scale=planes[:, g, :],
                    start=(g == 0),
                    stop=(g == PASSES - 1),
                )

        def rotate_alone(out, y, j):
            product = products.tile([P, 2 * GROUP_COLS], F32, name="product")
            nc.vector.tensor_tensor(
                out=product[:].rearrange("p (h i f e) -> p h i f e", h=GROUP_HEADS, f=2, e=2),
                in0=y.rearrange("p (h i e) -> p h i e", h=GROUP_HEADS, e=2).unsqueeze(3).to_broadcast([P, GROUP_HEADS, PAIRS, 2, 2]),
                in1=alone_pairs[:, j].unsqueeze(1).to_broadcast([P, GROUP_HEADS, PAIRS, 2, 2]),
                op=MULT,
            )
            nc.vector.tensor_reduce(
                out=out, in_=product[:].rearrange("p (h d e) -> p h d e", h=GROUP_HEADS, e=2), axis=mybir.AxisListType.X, op=ADD
            )

        def multiply_by_table(product, y, j, heads):
            nc.vector.tensor_tensor(
                out=product.rearrange("p e (h i f) -> p e h i f", h=heads, f=2),
                in0=y.rearrange("p (h i f) -> p h i f", h=heads, f=2).unsqueeze(1).to_broadcast([P, 2, heads, PAIRS, 2]),
                in1=table_pairs[:, j].unsqueeze(2).to_broadcast([P, 2, heads, PAIRS, 2]),
                op=MULT,
            )

        def add_products(out, product):
            nc.gpsimd.tensor_tensor(
                out=out,
                in0=product[:, 0, :].rearrange("p (h d) -> p h d", d=D),
                in1=product[:, 1, :].rearrange("p (x f) -> p x f", f=2)[:, :, ::-1],
                op=ADD,
            )

        def open_group(c):
            part = c // GROUPS_PER_PART
            turn = c % GROUPS_PER_PART
            n = [first <= c < end for first, end in LOADS].index(True)
            place = c - LOADS[n][0]
            words = w_words_sb[n][:, :, place * 2 * GROUP_COLS : (place + 1) * 2 * GROUP_COLS]
            m = [first <= c < end for first, end in PLANE_LOADS].index(True)
            place = c - PLANE_LOADS[m][0]
            planes = w_planes[m][:, :, place * GROUP_COLS : (place + 1) * GROUP_COLS]
            heads = outs[part][0, turn * GROUP_HEADS : (turn + 1) * GROUP_HEADS]
            runs = heads.rearrange("h (p j) d -> p h (j d)", j=TOKEN_TILES)
            stage = stages.tile([P, GROUP_HEADS, TOKEN_TILES, D], F32, name="stage")
            return words, planes, runs, stage

        def bank_of_tile(c, j, group):
            words, planes, runs, stage = group
            if (c, j) == (GROUP_ORDER[0], 0):
                heads = GROUP_HEADS // FIRST_HALVES
                for half in range(FIRST_HALVES):
                    acc = psum.tile([P, GROUP_COLS], F32, tag="bank")
                    for n in range(heads):
                        h = half * heads + n
                        multiply(
                            acc[:, n * D : (n + 1) * D], j, words[:, :, h * 2 * D : (h + 1) * 2 * D], planes[:, :, h * D : (h + 1) * D]
                        )
                    product = products.tile([P, 2, heads * D], F32, name="product")
                    multiply_by_table(product[:], acc[:, 0 : heads * D], j, heads)
                    add_products(stage[:, half * heads : (half + 1) * heads, j, :], product[:])
                return
            acc = psum.tile([P, GROUP_COLS], F32, tag="bank")
            multiply(acc[:], j, words, planes)
            if c >= 2 * GROUPS_PER_PART:
                nc.scalar.copy(out=stage[:, :, j, :], in_=acc[:].rearrange("p (h d) -> p h d", d=D))
            elif (c, j) in VECTOR_ALONE:
                rotate_alone(stage[:, :, j, :], acc[:], j)
            else:
                product = products.tile([P, 2, GROUP_COLS], F32, name="product")
                multiply_by_table(product[:], acc[:], j, GROUP_HEADS)
                add_products(stage[:, :, j, :], product[:])

        def store_group(group):
            words, planes, runs, stage = group
            nc.sync.dma_start(out=runs, in_=stage[:].rearrange("p h j d -> p h (j d)"))

        for j in range(TOKEN_TILES):
            quantise_tokens(j)
            keep_tensor_busy(1 if j == 1 else 2)
        computed = {}
        stored = 0
        for c in GROUP_ORDER:
            computed[c] = open_group(c)
            for j in range(TOKEN_TILES):
                bank_of_tile(c, j, computed[c])
            while stored < len(STORE_ORDER) and STORE_ORDER[stored] in computed:
                store_group(computed[STORE_ORDER[stored]])
                stored += 1
